import numpy as np
import ml_dtypes


def mxq(x, axis, fmt="e4m3"):
    dtype, down = {"e4m3": (ml_dtypes.float8_e4m3fn, 7), "e5m2": (ml_dtypes.float8_e5m2, 14)}[fmt]
    v = np.moveaxis(np.asarray(x, np.float32).astype(ml_dtypes.bfloat16).astype(np.float64), axis, -1)
    blocks = v.reshape(v.shape[:-1] + (-1, 32))
    amax = np.abs(blocks).max(-1, keepdims=True)
    byte = np.maximum(np.where(amax > 0, np.frexp(amax)[1] - 1 + 127, 0) - down, 1)
    scale = np.exp2(byte - 127.0)
    codes = (blocks / scale).astype(np.float32).astype(dtype).astype(np.float64)
    return np.moveaxis((codes * scale).reshape(v.shape), -1, axis)


WIDE = False


def mx_kscale(k):
    if not WIDE:
        return np.ones(k)
    levels = np.array([10, -10, 5, -5, 0])
    if k % 512:
        return np.exp2(np.random.permutation(np.resize(levels, k // 32))).repeat(32)
    a = np.empty((k // 512, 16))
    for p in range(k // 512):
        a[p, :8] = np.random.permutation(np.resize(levels, 8))
        for g in range(8):
            far = levels[np.abs(levels - a[p, g]) >= 10]
            a[p, g + 8] = far[np.random.randint(len(far))]
    return np.exp2(a.ravel()).repeat(32)


BF16 = ml_dtypes.bfloat16


def bf(x):
    return np.asarray(x, np.float32).astype(BF16)


def f64(x):
    return np.asarray(x).astype(np.float64)


B, C, D, O = 2, 256, 4096, 512
S0 = 1
S = 2
P = D // (S * (S0 + 1))
K = S * C


def setup_inputs():
    s = mx_kscale(K).reshape(S, C)
    sx = np.tile(np.repeat(s.T, S0 + 1, axis=1), (1, P))
    return {"x": bf(np.random.standard_normal((B, C, D)) * sx),
            "weight": bf(np.random.standard_normal((O, C, 1, S)) / C ** 0.25 / s.T[None, :, None, :])}


def reference(x, weight):
    xp = f64(x).reshape(B, C, D // (S0 + 1), S0 + 1).sum(axis=-1)
    xr = xp.reshape(B, C, P, S)
    a = xr.transpose(0, 2, 3, 1).reshape(B, P, K)
    w = f64(weight)[:, :, 0, :].transpose(2, 1, 0).reshape(K, O)
    out = (mxq(a, 2, "e4m3") @ mxq(w, 0, "e4m3")) / np.sqrt(C)
    return out.transpose(0, 2, 1)

@@ -1,0 +1,204 @@
+from contextlib import ExitStack
+
+import concourse.mybir as mybir
+from concourse.masks import make_identity
+
+BF16 = mybir.dt.bfloat16
+F32 = mybir.dt.float32
+U32 = mybir.dt.uint32
+I32 = mybir.dt.int32
+U8 = mybir.dt.uint8
+FP8X4 = mybir.dt.float8_e4m3fn_x4
+ADD = mybir.AluOpType.add
+COPY = mybir.ActivationFunctionType.Copy
+
+P = 128
+HALF = 64
+BATCH, CH, POS, OUTC = 2, 256, 4096, 512
+NPOS = POS // 4
+T = 4
+OT = OUTC // P
+FLOPS = 2 * BATCH * NPOS * (2 * CH) * OUTC
+INV = 1.0 / 16.0
+
+UNITS = [(0, 128), (128, 128), (256, 256), (512, 256), (768, 256)]
+HELP = {1: 64, 2: 64, 3: 64}
+HW = 64
+CW = 2 * P
+SW = CW + CW // 4
+W_ON_VECTOR = [1]
+ON_VECTOR = [(4, 1), (4, 3)]
+STORES = {1: (0, 256), 2: (256, 512), 3: (512, 768), 4: (768, 1024)}
+
+
+def tile_nonoverlappingconv1d_shared_kernel(tc, x, weight, out):
+    nc = tc.nc
+    with ExitStack() as ctx:
+        ctx.enter_context(tc.manual_schedule())
+        keep = ctx.enter_context(tc.tile_pool(name="keep", bufs=1))
+        psum_w = ctx.enter_context(tc.psum_pool(name="psum_w", bufs=2))
+        psum = ctx.enter_context(tc.psum_pool(name="psum", bufs=6))
+
+        w_sb = keep.tile([P, (OT + 1) * 2 * CH], BF16, name="w_sb")
+        nc.sync.dma_start(
+            out=w_sb[:, : OT * 2 * CH], in_=weight.rearrange("(p a) c one k -> p (a c one k)", a=OT)
+        )
+        x_view = x.rearrange("b (q t) d -> (b q) t d", t=T)
+        x_tiles = []
+        for u, (n0, w) in enumerate(UNITS):
+            xt = keep.tile([P, T, 4 * w], BF16, name="x%d" % u)
+            nc.sync.dma_start(out=xt[:], in_=x_view[:, :, 4 * n0 : 4 * (n0 + w)])
+            x_tiles.append(xt)
+
+        ident = keep.tile([P, P], F32, name="ident")
+        make_identity(nc, ident[:])
+        ident_b = keep.tile([P, P], BF16, name="ident_b")
+        make_identity(nc, ident_b[:])
+        warm_in = keep.tile([P, 1], F32, name="warm_in")
+        warm_out = keep.tile([P, 1], F32, name="warm_out")
+        nc.vector.memset(warm_in[:], 0.0)
+        nc.scalar.activation(out=warm_out[:], in_=warm_in[:], func=COPY, scale=1.0)
+        w_dup = keep.tile([P, OT * SW], U32, name="w_dup", align_bytes=64)
+        w_lo = keep.tile([P, OT * SW], U32, name="w_lo", align_bytes=64)
+        w_hi = keep.tile([P, OT * SW], U32, name="w_hi", align_bytes=64)
+        for s in range(OT):
+            nc.vector.memset(w_dup[:, s * SW + CW : (s + 1) * SW].bitcast(I32), 0)
+        nc.vector.memset(w_lo[HALF:P, :].bitcast(I32), 0)
+        nc.vector.memset(w_hi[0:HALF, :].bitcast(I32), 0)
+
+        nc.vector.tensor_copy(out=w_sb[:, OT * 2 * CH :], in_=w_sb[:, : 2 * CH])
+        w_words = w_sb[:].bitcast(F32)
+        w_grouped = keep.tile([P, OT * 4 * CW], BF16, name="w_grouped", align_bytes=64)
+
+        def w_transpose(s):
+            wT = psum_w.tile([P, 512], F32, name="wT")
+            for t in range(T):
+                c0 = s * CH + t
+                nc.tensor.transpose(wT[:, t * P : (t + 1) * P], w_words[:, c0 : c0 + 4 * P - 3 : 4], ident[:])
+            dst = w_grouped[:, s * 4 * CW : (s + 1) * 4 * CW].rearrange("p (k o t) -> p k o t", k=2, t=T)
+            src = wT[:].bitcast(BF16).rearrange("p (t o k) -> p k o t", t=T, k=2)
+            if s in W_ON_VECTOR:
+                nc.vector.tensor_copy(out=dst, in_=src)
+            else:
+                nc.scalar.copy(out=dst, in_=src)
+
+        def w_quant(s):
+            nc.vector.quantize_mx(
+                out=w_dup[:, s * SW : s * SW + CW].bitcast(FP8X4),
+                scales=w_dup[:, s * SW + CW : (s + 1) * SW].bitcast(U8),
+                in_=w_grouped[:, s * 4 * CW : (s + 1) * 4 * CW],
+            )
+
+        def w_move(s0, s1):
+            cols = slice(s0 * SW, s1 * SW)
+            nc.vector.tensor_copy(
+                out=w_lo[0:HALF, cols].bitcast(I32), in_=w_dup[0:HALF, cols].bitcast(I32)
+            )
+            nc.vector.tensor_copy(
+                out=w_hi[HALF:P, cols].bitcast(I32), in_=w_dup[HALF:P, cols].bitcast(I32)
+            )
+
+        def w_slot(b, a):
+            return (w_lo, a) if b == 0 else (w_hi, (a - 1) % OT)
+
+        out_sb = [keep.tile([P, OT, NPOS], F32, name="out_sb%d" % b) for b in range(BATCH)]
+        out_view = [out[b].rearrange("(p a) n -> p a n", a=OT) for b in range(BATCH)]
+        grouped = {}
+        codes = {}
+        scales = {}
+        for u, (n0, w) in enumerate(UNITS):
+            grouped[u] = keep.tile([P, 2 * w * T], BF16, name="g%d" % u, align_bytes=64)
+
+        def add(u):
+            n0, w = UNITS[u]
+            vw = w - HELP.get(u, 0)
+            src = x_tiles[u][:].rearrange("p t (n k e) -> p k n t e", k=2, e=2)[:, :, :vw]
+            dst = grouped[u][:].rearrange("p (k n t) -> p k n t", k=2, t=T)[:, :, :vw]
+            nc.vector.tensor_tensor(out=dst, in0=src[:, :, :, :, 0], in1=src[:, :, :, :, 1], op=ADD)
+
+        def help_add(u):
+            n0, w = UNITS[u]
+            vw = w - HW
+            hb = psum_w.tile([P, 512], F32, name="wT")
+            src = x_tiles[u][:, :, 4 * vw :].rearrange("p t (m e) -> p t m e", e=2)
+            for t in range(T):
+                for e in range(2):
+                    nc.tensor.matmul(
+                        out=hb[:, t * 2 * HW : (t + 1) * 2 * HW],
+                        lhsT=ident_b[:],
+                        rhs=src[:, t, :, e],
+                        start=(e == 0),
+                        stop=(e == 1),
+                    )
+            nc.scalar.copy(
+                out=grouped[u][:].rearrange("p (k n t) -> p k n t", k=2, t=T)[:, :, vw:],
+                in_=hb[:].rearrange("p (t n k) -> p k n t", t=T, k=2),
+            )
+
+        def quant(u):
+            w = UNITS[u][1]
+            c = keep.tile([P, 2 * w], U32, name="c%d" % u, align_bytes=64)
+            s = keep.tile([P, 2 * w], U8, name="s%d" % u, align_bytes=64)
+            nc.vector.quantize_mx(out=c[:].bitcast(FP8X4), scales=s[:], in_=grouped[u][:])
+            codes[u] = c
+            scales[u] = s
+
+        def multiply(u):
+            n0, w = UNITS[u]
+            ga = 512 // w
+            i = 0
+            for a0 in range(0, OT, ga):
+                for b in range(BATCH):
+                    acc = psum.tile([P, 512], F32, name="acc")
+                    for j in range(ga):
+                        wt, s = w_slot(b, a0 + j)
+                        base = s * SW
+                        sc = wt[:, base + CW : base + SW].bitcast(U8)
+                        for k in range(2):
+                            nc.tensor.matmul_mx(
+                                out=acc[:, j * w : (j + 1) * w],
+                                lhsT=wt[:, base + k * P : base + (k + 1) * P].bitcast(FP8X4),
+                                lhsT_scale=sc[:, k * P : (k + 1) * P],
+                                rhs=codes[u][:, k * w : (k + 1) * w].bitcast(FP8X4),
+                                rhs_scale=scales[u][:, k * w : (k + 1) * w],
+                                start=(k == 0),
+                                stop=(k == 1),
+                            )
+                    dst = out_sb[b][:, a0 : a0 + ga, n0 : n0 + w]
+                    srcv = acc[:].rearrange("p (a n) -> p a n", a=ga)
+                    if (u, i) in ON_VECTOR:
+                        nc.vector.tensor_scalar_mul(out=dst, in0=srcv, scalar1=INV)
+                    else:
+                        nc.scalar.activation(out=dst, in_=srcv, func=COPY, scale=INV)
+                    i += 1
+            if u in STORES:
+                s0, s1 = STORES[u]
+                for b in range(BATCH):
+                    nc.sync.dma_start(out=out_view[b][:, :, s0:s1], in_=out_sb[b][:, :, s0:s1])
+
+        for s in range(OT):
+            w_transpose(s)
+        add(0)
+        w_quant(0)
+        w_quant(1)
+        w_move(0, 2)
+        quant(0)
+        help_add(1)
+        w_quant(2)
+        w_quant(3)
+        w_move(2, 4)
+        add(1)
+        multiply(0)
+        help_add(2)
+        add(2)
+        quant(1)
+        multiply(1)
+        add(3)
+        help_add(3)
+        quant(2)
+        multiply(2)
+        add(4)
+        quant(3)
+        multiply(3)
+        quant(4)
+        multiply(4)

@@ -75,8 +75,8 @@ def tile_nonoverlappingconv1d_shared_kernel(tc, x, weight, out):
             for t in range(T):
                 c0 = s * CH + t
                 nc.tensor.transpose(wT[:, t * P : (t + 1) * P], w_words[:, c0 : c0 + 4 * P - 3 : 4], ident[:])
-            dst = w_grouped[:, s * 4 * CW : (s + 1) * 4 * CW].rearrange("p (k o t) -> p k o t", k=2, t=T)
-            src = wT[:].bitcast(BF16).rearrange("p (t o k) -> p k o t", t=T, k=2)
+            dst = w_grouped[:, s * 4 * CW : (s + 1) * 4 * CW].rearrange("p (k o t) -> p o k t", k=2, t=T)
+            src = wT[:].bitcast(BF16).rearrange("p (t o k) -> p o k t", t=T, k=2)
             if s in W_ON_VECTOR:
                 nc.vector.tensor_copy(out=dst, in_=src)
             else:
@@ -112,8 +112,8 @@ def tile_nonoverlappingconv1d_shared_kernel(tc, x, weight, out):
         def add(u):
             n0, w = UNITS[u]
             vw = w - HELP.get(u, 0)
-            src = x_tiles[u][:].rearrange("p t (n k e) -> p k n t e", k=2, e=2)[:, :, :vw]
-            dst = grouped[u][:].rearrange("p (k n t) -> p k n t", k=2, t=T)[:, :, :vw]
+            src = x_tiles[u][:].rearrange("p t (n k e) -> p n k t e", k=2, e=2)[:, :vw]
+            dst = grouped[u][:].rearrange("p (k n t) -> p n k t", k=2, t=T)[:, :vw]
             nc.vector.tensor_tensor(out=dst, in0=src[:, :, :, :, 0], in1=src[:, :, :, :, 1], op=ADD)
 
         def help_add(u):
@@ -131,8 +131,8 @@ def tile_nonoverlappingconv1d_shared_kernel(tc, x, weight, out):
                         stop=(e == 1),
                     )
             nc.scalar.copy(
-                out=grouped[u][:].rearrange("p (k n t) -> p k n t", k=2, t=T)[:, :, vw:],
-                in_=hb[:].rearrange("p (t n k) -> p k n t", t=T, k=2),
+                out=grouped[u][:].rearrange("p (k n t) -> p n k t", k=2, t=T)[:, vw:],
+                in_=hb[:].rearrange("p (t n k) -> p n k t", t=T, k=2),
             )
 
         def quant(u):

@@ -75,8 +75,8 @@ def tile_nonoverlappingconv1d_shared_kernel(tc, x, weight, out):
             for t in range(T):
                 c0 = s * CH + t
                 nc.tensor.transpose(wT[:, t * P : (t + 1) * P], w_words[:, c0 : c0 + 4 * P - 3 : 4], ident[:])
-            dst = w_grouped[:, s * 4 * CW : (s + 1) * 4 * CW].rearrange("p (k o t) -> p o k t", k=2, t=T)
-            src = wT[:].bitcast(BF16).rearrange("p (t o k) -> p o k t", t=T, k=2)
+            dst = w_grouped[:, s * 4 * CW : (s + 1) * 4 * CW].rearrange("p (k o t) -> p o t k", k=2, t=T)
+            src = wT[:].bitcast(BF16).rearrange("p (t o k) -> p o t k", t=T, k=2)
             if s in W_ON_VECTOR:
                 nc.vector.tensor_copy(out=dst, in_=src)
             else:
@@ -112,8 +112,8 @@ def tile_nonoverlappingconv1d_shared_kernel(tc, x, weight, out):
         def add(u):
             n0, w = UNITS[u]
             vw = w - HELP.get(u, 0)
-            src = x_tiles[u][:].rearrange("p t (n k e) -> p n k t e", k=2, e=2)[:, :vw]
-            dst = grouped[u][:].rearrange("p (k n t) -> p n k t", k=2, t=T)[:, :vw]
+            src = x_tiles[u][:].rearrange("p t (n k e) -> p n t k e", k=2, e=2)[:, :vw]
+            dst = grouped[u][:].rearrange("p (k n t) -> p n t k", k=2, t=T)[:, :vw]
             nc.vector.tensor_tensor(out=dst, in0=src[:, :, :, :, 0], in1=src[:, :, :, :, 1], op=ADD)
 
         def help_add(u):
@@ -131,8 +131,8 @@ def tile_nonoverlappingconv1d_shared_kernel(tc, x, weight, out):
                         stop=(e == 1),
                     )
             nc.scalar.copy(
-                out=grouped[u][:].rearrange("p (k n t) -> p n k t", k=2, t=T)[:, vw:],
-                in_=hb[:].rearrange("p (t n k) -> p n k t", t=T, k=2),
+                out=grouped[u][:].rearrange("p (k n t) -> p n t k", k=2, t=T)[:, vw:],
+                in_=hb[:].rearrange("p (t n k) -> p n t k", t=T, k=2),
             )
 
         def quant(u):

@@ -21,14 +21,12 @@ OT = OUTC // P
 FLOPS = 2 * BATCH * NPOS * (2 * CH) * OUTC
 INV = 1.0 / 16.0
 
-UNITS = [(0, 128), (128, 128), (256, 256), (512, 256), (768, 256)]
-HELP = {1: 64, 2: 64, 3: 64}
+W = 128
+NU = NPOS // W
+LOADS = [(0, 128), (128, 256), (384, 256), (640, 256), (896, 128)]
 HW = 64
 CW = 2 * P
 SW = CW + CW // 4
-W_ON_VECTOR = [1]
-ON_VECTOR = [(4, 1), (4, 3)]
-STORES = {1: (0, 256), 2: (256, 512), 3: (512, 768), 4: (768, 1024)}
 
 
 def tile_nonoverlappingconv1d_shared_kernel(tc, x, weight, out):
@@ -39,16 +37,22 @@ def tile_nonoverlappingconv1d_shared_kernel(tc, x, weight, out):
         psum_w = ctx.enter_context(tc.psum_pool(name="psum_w", bufs=2))
         psum = ctx.enter_context(tc.psum_pool(name="psum", bufs=6))
 
-        w_sb = keep.tile([P, (OT + 1) * 2 * CH], BF16, name="w_sb")
-        nc.sync.dma_start(
-            out=w_sb[:, : OT * 2 * CH], in_=weight.rearrange("(p a) c one k -> p (a c one k)", a=OT)
-        )
+        w_sb = keep.tile([P, OT * 2 * CH], BF16, name="w_sb")
+        w_view = weight.rearrange("(p a) c one k -> p (a c one k)", a=OT)
+        for h in range(2):
+            cols = slice(h * OT * CH, (h + 1) * OT * CH)
+            nc.sync.dma_start(out=w_sb[:, cols], in_=w_view[:, cols])
         x_view = x.rearrange("b (q t) d -> (b q) t d", t=T)
         x_tiles = []
-        for u, (n0, w) in enumerate(UNITS):
-            xt = keep.tile([P, T, 4 * w], BF16, name="x%d" % u)
+        for i, (n0, w) in enumerate(LOADS):
+            xt = keep.tile([P, T, 4 * w], BF16, name="x%d" % i)
             nc.sync.dma_start(out=xt[:], in_=x_view[:, :, 4 * n0 : 4 * (n0 + w)])
             x_tiles.append(xt)
+
+        def x_part(n0, w):
+            i = [j for j, (l0, lw) in enumerate(LOADS) if l0 <= n0 < l0 + lw][0]
+            off = 4 * (n0 - LOADS[i][0])
+            return x_tiles[i][:, :, off : off + 4 * w]
 
         ident = keep.tile([P, P], F32, name="ident")
         make_identity(nc, ident[:])
@@ -63,24 +67,34 @@ def tile_nonoverlappingconv1d_shared_kernel(tc, x, weight, out):
         w_hi = keep.tile([P, OT * SW], U32, name="w_hi", align_bytes=64)
         for s in range(OT):
             nc.vector.memset(w_dup[:, s * SW + CW : (s + 1) * SW].bitcast(I32), 0)
-        nc.vector.memset(w_lo[HALF:P, :].bitcast(I32), 0)
-        nc.vector.memset(w_hi[0:HALF, :].bitcast(I32), 0)
+        nc.gpsimd.memset(w_lo[HALF:P, :].bitcast(I32), 0)
+        nc.gpsimd.memset(w_hi[0:HALF, :].bitcast(I32), 0)
 
-        nc.vector.tensor_copy(out=w_sb[:, OT * 2 * CH :], in_=w_sb[:, : 2 * CH])
-        w_words = w_sb[:].bitcast(F32)
+        wk = [keep.tile([P, 2, 2, 3 * P], BF16, name="wk%d" % h) for h in range(2)]
+
+        def w_split(copy, h, t0, t1, at):
+            for k in range(2):
+                copy(
+                    out=wk[h][:, k, :, at * P : (at + t1 - t0) * P].rearrange("p e (m i) -> p m e i", i=2),
+                    in_=w_sb[:, (2 * h + t0) * 2 * CH : (2 * h + t1) * 2 * CH].rearrange(
+                        "p (m e i k) -> p k m e i", e=2, i=2, k=2
+                    )[:, k],
+                )
+
         w_grouped = keep.tile([P, OT * 4 * CW], BF16, name="w_grouped", align_bytes=64)
+        wg_words = w_grouped[:].bitcast(F32)
 
         def w_transpose(s):
+            h, j = divmod(s, 2)
+            words = wk[h][:].rearrange("p k e c -> p (k e c)").bitcast(F32)
             wT = psum_w.tile([P, 512], F32, name="wT")
-            for t in range(T):
-                c0 = s * CH + t
-                nc.tensor.transpose(wT[:, t * P : (t + 1) * P], w_words[:, c0 : c0 + 4 * P - 3 : 4], ident[:])
-            dst = w_grouped[:, s * 4 * CW : (s + 1) * 4 * CW].rearrange("p (k o t) -> p o t k", k=2, t=T)
-            src = wT[:].bitcast(BF16).rearrange("p (t o k) -> p o t k", t=T, k=2)
-            if s in W_ON_VECTOR:
-                nc.vector.tensor_copy(out=dst, in_=src)
-            else:
-                nc.scalar.copy(out=dst, in_=src)
+            for r in range(4):
+                c0 = r * 3 * HALF + j * HALF
+                nc.tensor.transpose(wT[:, r * P : (r + 1) * P], words[:, c0 : c0 + P], ident[:])
+            nc.scalar.copy(
+                out=wg_words[:, s * 512 : (s + 1) * 512].rearrange("p (k o e) -> p k o e", k=2, e=2),
+                in_=wT[:].rearrange("p (k e o) -> p k o e", k=2, e=2),
+            )
 
         def w_quant(s):
             nc.vector.quantize_mx(
@@ -99,28 +113,35 @@ def tile_nonoverlappingconv1d_shared_kernel(tc, x, weight, out):
             )
 
         def w_slot(b, a):
-            return (w_lo, a) if b == 0 else (w_hi, (a - 1) % OT)
+            return (w_lo, a) if b == 0 else (w_hi, a ^ 1)
 
         out_sb = [keep.tile([P, OT, NPOS], F32, name="out_sb%d" % b) for b in range(BATCH)]
         out_view = [out[b].rearrange("(p a) n -> p a n", a=OT) for b in range(BATCH)]
-        grouped = {}
-        codes = {}
-        scales = {}
-        for u, (n0, w) in enumerate(UNITS):
-            grouped[u] = keep.tile([P, 2 * w * T], BF16, name="g%d" % u, align_bytes=64)
+        grouped = []
+        codes = []
+        scales = []
+        for u in range(NU):
+            g = keep.tile([P, 2 * W * T], BF16, name="g%d" % u, align_bytes=64)
+            c = keep.tile([P, 2 * W], U32, name="c%d" % u, align_bytes=64)
+            s = keep.tile([P, 2 * W], U8, name="s%d" % u, align_bytes=64)
+            grouped.append(g)
+            codes.append(c)
+            scales.append(s)
 
-        def add(u):
-            n0, w = UNITS[u]
-            vw = w - HELP.get(u, 0)
-            src = x_tiles[u][:].rearrange("p t (n k e) -> p n t k e", k=2, e=2)[:, :vw]
-            dst = grouped[u][:].rearrange("p (k n t) -> p n t k", k=2, t=T)[:, :vw]
-            nc.vector.tensor_tensor(out=dst, in0=src[:, :, :, :, 0], in1=src[:, :, :, :, 1], op=ADD)
+        def add(n0, w):
+            u, i = divmod(n0, W)
+            src = x_part(n0, w).rearrange("p t (n k e) -> p n t k e", k=2, e=2)
+            nc.vector.tensor_tensor(
+                out=grouped[u][:].rearrange("p (k n t) -> p n t k", k=2, t=T)[:, i : i + w],
+                in0=src[:, :, :, :, 0],
+                in1=src[:, :, :, :, 1],
+                op=ADD,
+            )
 
-        def help_add(u):
-            n0, w = UNITS[u]
-            vw = w - HW
+        def help_add(n0):
+            u, i = divmod(n0, W)
             hb = psum_w.tile([P, 512], F32, name="wT")
-            src = x_tiles[u][:, :, 4 * vw :].rearrange("p t (m e) -> p t m e", e=2)
+            src = x_part(n0, HW).rearrange("p t (m e) -> p t m e", e=2)
             for t in range(T):
                 for e in range(2):
                     nc.tensor.matmul(
@@ -131,74 +152,84 @@ def tile_nonoverlappingconv1d_shared_kernel(tc, x, weight, out):
                         stop=(e == 1),
                     )
             nc.scalar.copy(
-                out=grouped[u][:].rearrange("p (k n t) -> p n t k", k=2, t=T)[:, vw:],
+                out=grouped[u][:].rearrange("p (k n t) -> p n t k", k=2, t=T)[:, i : i + HW],
                 in_=hb[:].rearrange("p (t n k) -> p n t k", t=T, k=2),
             )
 
         def quant(u):
-            w = UNITS[u][1]
-            c = keep.tile([P, 2 * w], U32, name="c%d" % u, align_bytes=64)
-            s = keep.tile([P, 2 * w], U8, name="s%d" % u, align_bytes=64)
-            nc.vector.quantize_mx(out=c[:].bitcast(FP8X4), scales=s[:], in_=grouped[u][:])
-            codes[u] = c
-            scales[u] = s
+            nc.vector.quantize_mx(out=codes[u][:].bitcast(FP8X4), scales=scales[u][:], in_=grouped[u][:])
 
-        def multiply(u):
-            n0, w = UNITS[u]
-            ga = 512 // w
-            i = 0
-            for a0 in range(0, OT, ga):
-                for b in range(BATCH):
-                    acc = psum.tile([P, 512], F32, name="acc")
-                    for j in range(ga):
-                        wt, s = w_slot(b, a0 + j)
-                        base = s * SW
-                        sc = wt[:, base + CW : base + SW].bitcast(U8)
-                        for k in range(2):
-                            nc.tensor.matmul_mx(
-                                out=acc[:, j * w : (j + 1) * w],
-                                lhsT=wt[:, base + k * P : base + (k + 1) * P].bitcast(FP8X4),
-                                lhsT_scale=sc[:, k * P : (k + 1) * P],
-                                rhs=codes[u][:, k * w : (k + 1) * w].bitcast(FP8X4),
-                                rhs_scale=scales[u][:, k * w : (k + 1) * w],
-                                start=(k == 0),
-                                stop=(k == 1),
-                            )
-                    dst = out_sb[b][:, a0 : a0 + ga, n0 : n0 + w]
-                    srcv = acc[:].rearrange("p (a n) -> p a n", a=ga)
-                    if (u, i) in ON_VECTOR:
-                        nc.vector.tensor_scalar_mul(out=dst, in0=srcv, scalar1=INV)
-                    else:
-                        nc.scalar.activation(out=dst, in_=srcv, func=COPY, scale=INV)
-                    i += 1
-            if u in STORES:
-                s0, s1 = STORES[u]
-                for b in range(BATCH):
-                    nc.sync.dma_start(out=out_view[b][:, :, s0:s1], in_=out_sb[b][:, :, s0:s1])
+        def bank(u, b, tiles, on_vector=False):
+            acc = psum.tile([P, 512], F32, name="acc")
+            for j, a in enumerate(tiles):
+                wt, s = w_slot(b, a)
+                base = s * SW
+                sc = wt[:, base + CW : base + SW].bitcast(U8)
+                for k in range(2):
+                    nc.tensor.matmul_mx(
+                        out=acc[:, j * W : (j + 1) * W],
+                        lhsT=wt[:, base + k * P : base + (k + 1) * P].bitcast(FP8X4),
+                        lhsT_scale=sc[:, k * P : (k + 1) * P],
+                        rhs=codes[u][:, k * W : (k + 1) * W].bitcast(FP8X4),
+                        rhs_scale=scales[u][:, k * W : (k + 1) * W],
+                        start=(k == 0),
+                        stop=(k == 1),
+                    )
+            dst = out_sb[b][:, tiles[0] : tiles[-1] + 1, u * W : (u + 1) * W]
+            srcv = acc[:, : len(tiles) * W].rearrange("p (a n) -> p a n", n=W)
+            if on_vector:
+                nc.vector.tensor_scalar_mul(out=dst, in0=srcv, scalar1=INV)
+            else:
+                nc.scalar.activation(out=dst, in_=srcv, func=COPY, scale=INV)
 
+        def store(b, u0, u1):
+            n = slice(u0 * W, u1 * W)
+            nc.sync.dma_start(out=out_view[b][:, :, n], in_=out_sb[b][:, :, n])
+
+        ALL = [0, 1, 2, 3]
+        for h in range(2):
+            w_split(nc.vector.tensor_copy, h, 0, 2, 0)
+            w_split(nc.scalar.copy, h, 0, 1, 2)
         for s in range(OT):
             w_transpose(s)
-        add(0)
+        add(0, W)
         w_quant(0)
         w_quant(1)
         w_move(0, 2)
         quant(0)
-        help_add(1)
+        bank(0, 0, [0, 1])
+        bank(0, 1, [0, 1])
+        help_add(128)
         w_quant(2)
         w_quant(3)
+        help_add(192)
         w_move(2, 4)
-        add(1)
-        multiply(0)
-        help_add(2)
-        add(2)
+        add(256, W)
+        bank(0, 0, [2, 3])
+        store(0, 0, 1)
+        bank(0, 1, [2, 3])
+        store(1, 0, 1)
         quant(1)
-        multiply(1)
-        add(3)
-        help_add(3)
+        help_add(384)
+        add(448, 64)
+        bank(1, 0, ALL)
+        bank(1, 1, ALL)
         quant(2)
-        multiply(2)
-        add(4)
-        quant(3)
-        multiply(3)
-        quant(4)
-        multiply(4)
+        for u in range(2, NU - 1):
+            if u < NU - 3:
+                add((u + 2) * W, W)
+            elif u == NU - 3:
+                add((u + 2) * W, W // 2)
+            else:
+                add((u + 1) * W + W // 2, W // 2)
+            quant(u + 1)
+            bank(u, 0, ALL, u == NU - 2)
+            if u % 2 == 0:
+                store(0, u - 1, u + 1)
+            bank(u, 1, ALL)
+            if u % 2 == 0:
+                store(1, u - 1, u + 1)
+        bank(NU - 1, 0, ALL, True)
+        store(0, NU - 1, NU)
+        bank(NU - 1, 1, ALL)
+        store(1, NU - 1, NU)

@@ -62,22 +62,20 @@ def tile_nonoverlappingconv1d_shared_kernel(tc, x, weight, out):
         warm_out = keep.tile([P, 1], F32, name="warm_out")
         nc.vector.memset(warm_in[:], 0.0)
         nc.scalar.activation(out=warm_out[:], in_=warm_in[:], func=COPY, scale=1.0)
-        w_dup = keep.tile([P, OT * SW], U32, name="w_dup", align_bytes=64)
         w_lo = keep.tile([P, OT * SW], U32, name="w_lo", align_bytes=64)
         w_hi = keep.tile([P, OT * SW], U32, name="w_hi", align_bytes=64)
         for s in range(OT):
-            nc.vector.memset(w_dup[:, s * SW + CW : (s + 1) * SW].bitcast(I32), 0)
+            nc.vector.memset(w_hi[:, s * SW + CW : (s + 1) * SW].bitcast(I32), 0)
         nc.gpsimd.memset(w_lo[HALF:P, :].bitcast(I32), 0)
-        nc.gpsimd.memset(w_hi[0:HALF, :].bitcast(I32), 0)
 
         wk = [keep.tile([P, 2, 2, 3 * P], BF16, name="wk%d" % h) for h in range(2)]
 
         def w_split(copy, h, t0, t1, at):
             for k in range(2):
                 copy(
-                    out=wk[h][:, k, :, at * P : (at + t1 - t0) * P].rearrange("p e (m i) -> p m e i", i=2),
+                    out=wk[h][:, k, :, at * P : (at + t1 - t0) * P].rearrange("p e (m i) -> p e m i", i=2),
                     in_=w_sb[:, (2 * h + t0) * 2 * CH : (2 * h + t1) * 2 * CH].rearrange(
-                        "p (m e i k) -> p k m e i", e=2, i=2, k=2
+                        "p (m e i k) -> p k e m i", e=2, i=2, k=2
                     )[:, k],
                 )
 
@@ -98,19 +96,17 @@ def tile_nonoverlappingconv1d_shared_kernel(tc, x, weight, out):
 
         def w_quant(s):
             nc.vector.quantize_mx(
-                out=w_dup[:, s * SW : s * SW + CW].bitcast(FP8X4),
-                scales=w_dup[:, s * SW + CW : (s + 1) * SW].bitcast(U8),
+                out=w_hi[:, s * SW : s * SW + CW].bitcast(FP8X4),
+                scales=w_hi[:, s * SW + CW : (s + 1) * SW].bitcast(U8),
                 in_=w_grouped[:, s * 4 * CW : (s + 1) * 4 * CW],
             )
 
         def w_move(s0, s1):
             cols = slice(s0 * SW, s1 * SW)
             nc.vector.tensor_copy(
-                out=w_lo[0:HALF, cols].bitcast(I32), in_=w_dup[0:HALF, cols].bitcast(I32)
+                out=w_lo[0:HALF, cols].bitcast(I32), in_=w_hi[0:HALF, cols].bitcast(I32)
             )
-            nc.vector.tensor_copy(
-                out=w_hi[HALF:P, cols].bitcast(I32), in_=w_dup[HALF:P, cols].bitcast(I32)
-            )
+            nc.gpsimd.memset(w_hi[0:HALF, cols].bitcast(I32), 0)
 
         def w_slot(b, a):
             return (w_lo, a) if b == 0 else (w_hi, a ^ 1)
@@ -209,9 +205,9 @@ def tile_nonoverlappingconv1d_shared_kernel(tc, x, weight, out):
         store(0, 0, 1)
         bank(0, 1, [2, 3])
         store(1, 0, 1)
+        add(448, 64)
         quant(1)
         help_add(384)
-        add(448, 64)
         bank(1, 0, ALL)
         bank(1, 1, ALL)
         quant(2)

@@ -68,27 +68,26 @@ def tile_nonoverlappingconv1d_shared_kernel(tc, x, weight, out):
             nc.vector.memset(w_hi[:, s * SW + CW : (s + 1) * SW].bitcast(I32), 0)
         nc.gpsimd.memset(w_lo[HALF:P, :].bitcast(I32), 0)
 
-        wk = [keep.tile([P, 2, 2, 3 * P], BF16, name="wk%d" % h) for h in range(2)]
+        wk = [keep.tile([P, 2, 3 * CH], BF16, name="wk%d" % h) for h in range(2)]
 
         def w_split(copy, h, t0, t1, at):
-            for k in range(2):
-                copy(
-                    out=wk[h][:, k, :, at * P : (at + t1 - t0) * P].rearrange("p e (m i) -> p e m i", i=2),
-                    in_=w_sb[:, (2 * h + t0) * 2 * CH : (2 * h + t1) * 2 * CH].rearrange(
-                        "p (m e i k) -> p k e m i", e=2, i=2, k=2
-                    )[:, k],
-                )
+            copy(
+                out=wk[h][:, :, at * CH : (at + t1 - t0) * CH],
+                in_=w_sb[:, (2 * h + t0) * 2 * CH : (2 * h + t1) * 2 * CH].rearrange("p (c k) -> p k c", k=2),
+            )
 
         w_grouped = keep.tile([P, OT * 4 * CW], BF16, name="w_grouped", align_bytes=64)
         wg_words = w_grouped[:].bitcast(F32)
 
         def w_transpose(s):
             h, j = divmod(s, 2)
-            words = wk[h][:].rearrange("p k e c -> p (k e c)").bitcast(F32)
+            words = wk[h][:].rearrange("p k c -> p (k c)").bitcast(F32)
             wT = psum_w.tile([P, 512], F32, name="wT")
-            for r in range(4):
-                c0 = r * 3 * HALF + j * HALF
-                nc.tensor.transpose(wT[:, r * P : (r + 1) * P], words[:, c0 : c0 + P], ident[:])
+            for k in range(2):
+                for e in range(2):
+                    c0 = k * 3 * P + j * P + e
+                    col = (2 * k + e) * P
+                    nc.tensor.transpose(wT[:, col : col + P], words[:, c0 : c0 + 2 * P - 1 : 2], ident[:])
             nc.scalar.copy(
                 out=wg_words[:, s * 512 : (s + 1) * 512].rearrange("p (k o e) -> p k o e", k=2, e=2),
                 in_=wT[:].rearrange("p (k e o) -> p k o e", k=2, e=2),

@@ -23,7 +23,8 @@ INV = 1.0 / 16.0
 
 W = 128
 NU = NPOS // W
-LOADS = [(0, 128), (128, 256), (384, 256), (640, 256), (896, 128)]
+LOADS = [(0, 128), (128, 128), (256, 256), (512, 128), (640, 128), (768, 256)]
+EARLY = 4
 HW = 64
 CW = 2 * P
 SW = CW + CW // 4
@@ -46,8 +47,14 @@ def tile_nonoverlappingconv1d_shared_kernel(tc, x, weight, out):
         x_tiles = []
         for i, (n0, w) in enumerate(LOADS):
             xt = keep.tile([P, T, 4 * w], BF16, name="x%d" % i)
-            nc.sync.dma_start(out=xt[:], in_=x_view[:, :, 4 * n0 : 4 * (n0 + w)])
             x_tiles.append(xt)
+
+        def load_x(i):
+            n0, w = LOADS[i]
+            nc.sync.dma_start(out=x_tiles[i][:], in_=x_view[:, :, 4 * n0 : 4 * (n0 + w)])
+
+        for i in range(EARLY):
+            load_x(i)
 
         def x_part(n0, w):
             i = [j for j, (l0, lw) in enumerate(LOADS) if l0 <= n0 < l0 + lw][0]
@@ -64,51 +71,57 @@ def tile_nonoverlappingconv1d_shared_kernel(tc, x, weight, out):
         nc.scalar.activation(out=warm_out[:], in_=warm_in[:], func=COPY, scale=1.0)
         w_lo = keep.tile([P, OT * SW], U32, name="w_lo", align_bytes=64)
         w_hi = keep.tile([P, OT * SW], U32, name="w_hi", align_bytes=64)
-        for s in range(OT):
-            nc.vector.memset(w_hi[:, s * SW + CW : (s + 1) * SW].bitcast(I32), 0)
+        w_q = keep.tile([P, 2 * SW], U32, name="w_q", align_bytes=64)
+        for j in range(2):
+            nc.vector.memset(w_q[:, j * SW + CW : (j + 1) * SW].bitcast(I32), 0)
         nc.gpsimd.memset(w_lo[HALF:P, :].bitcast(I32), 0)
+        nc.gpsimd.memset(w_hi[0:HALF, :].bitcast(I32), 0)
 
-        wk = [keep.tile([P, 2, 3 * CH], BF16, name="wk%d" % h) for h in range(2)]
+        wk = [keep.tile([P, 2, 2 * CH], BF16, name="wk%d" % j) for j in range(2)]
 
-        def w_split(copy, h, t0, t1, at):
+        def w_split(copy, j, t0, t1):
             copy(
-                out=wk[h][:, :, at * CH : (at + t1 - t0) * CH],
-                in_=w_sb[:, (2 * h + t0) * 2 * CH : (2 * h + t1) * 2 * CH].rearrange("p (c k) -> p k c", k=2),
+                out=wk[j][:, :, t0 * CH : t1 * CH],
+                in_=w_sb[:, (2 * j + t0) * 2 * CH : (2 * j + t1) * 2 * CH].rearrange("p (c k) -> p k c", k=2),
             )
 
-        w_grouped = keep.tile([P, OT * 4 * CW], BF16, name="w_grouped", align_bytes=64)
+        w_grouped = keep.tile([P, 2 * 4 * CW], BF16, name="w_grouped", align_bytes=64)
         wg_words = w_grouped[:].bitcast(F32)
 
-        def w_transpose(s):
-            h, j = divmod(s, 2)
-            words = wk[h][:].rearrange("p k c -> p (k c)").bitcast(F32)
+        def w_transpose(j):
+            words = wk[j][:].rearrange("p k c -> p (k c)").bitcast(F32)
             wT = psum_w.tile([P, 512], F32, name="wT")
             for k in range(2):
                 for e in range(2):
-                    c0 = k * 3 * P + j * P + e
+                    c0 = k * 2 * P + e
                     col = (2 * k + e) * P
                     nc.tensor.transpose(wT[:, col : col + P], words[:, c0 : c0 + 2 * P - 1 : 2], ident[:])
             nc.scalar.copy(
-                out=wg_words[:, s * 512 : (s + 1) * 512].rearrange("p (k o e) -> p k o e", k=2, e=2),
+                out=wg_words[:, j * 512 : (j + 1) * 512].rearrange("p (k o e) -> p k o e", k=2, e=2),
                 in_=wT[:].rearrange("p (k e o) -> p k o e", k=2, e=2),
             )
 
-        def w_quant(s):
+        def w_quant(j):
             nc.vector.quantize_mx(
-                out=w_hi[:, s * SW : s * SW + CW].bitcast(FP8X4),
-                scales=w_hi[:, s * SW + CW : (s + 1) * SW].bitcast(U8),
-                in_=w_grouped[:, s * 4 * CW : (s + 1) * 4 * CW],
+                out=w_q[:, j * SW : j * SW + CW].bitcast(FP8X4),
+                scales=w_q[:, j * SW + CW : (j + 1) * SW].bitcast(U8),
+                in_=w_grouped[:, j * 4 * CW : (j + 1) * 4 * CW],
             )
 
-        def w_move(s0, s1):
-            cols = slice(s0 * SW, s1 * SW)
-            nc.vector.tensor_copy(
-                out=w_lo[0:HALF, cols].bitcast(I32), in_=w_hi[0:HALF, cols].bitcast(I32)
-            )
-            nc.gpsimd.memset(w_hi[0:HALF, cols].bitcast(I32), 0)
+        def w_move():
+            even = slice(0, 2 * SW)
+            odd = slice(2 * SW, 4 * SW)
+            nc.sync.dma_start(out=w_lo[0:HALF, odd].bitcast(I32), in_=w_q[HALF:P, :].bitcast(I32))
+            nc.sync.dma_start(out=w_hi[HALF:P, even].bitcast(I32), in_=w_q[0:HALF, :].bitcast(I32))
+
+        def w_keep():
+            even = slice(0, 2 * SW)
+            odd = slice(2 * SW, 4 * SW)
+            nc.vector.tensor_copy(out=w_lo[0:HALF, even].bitcast(I32), in_=w_q[0:HALF, :].bitcast(I32))
+            nc.vector.tensor_copy(out=w_hi[HALF:P, odd].bitcast(I32), in_=w_q[HALF:P, :].bitcast(I32))
 
         def w_slot(b, a):
-            return (w_lo, a) if b == 0 else (w_hi, a ^ 1)
+            return (w_lo if b == 0 else w_hi), 2 * (a % 2) + a // 2
 
         out_sb = [keep.tile([P, OT, NPOS], F32, name="out_sb%d" % b) for b in range(BATCH)]
         out_view = [out[b].rearrange("(p a) n -> p a n", a=OT) for b in range(BATCH)]
@@ -170,7 +183,8 @@ def tile_nonoverlappingconv1d_shared_kernel(tc, x, weight, out):
                         start=(k == 0),
                         stop=(k == 1),
                     )
-            dst = out_sb[b][:, tiles[0] : tiles[-1] + 1, u * W : (u + 1) * W]
+            step = tiles[1] - tiles[0]
+            dst = out_sb[b][:, tiles[0] : tiles[-1] + 1 : step, u * W : (u + 1) * W]
             srcv = acc[:, : len(tiles) * W].rearrange("p (a n) -> p a n", n=W)
             if on_vector:
                 nc.vector.tensor_scalar_mul(out=dst, in0=srcv, scalar1=INV)
@@ -182,49 +196,42 @@ def tile_nonoverlappingconv1d_shared_kernel(tc, x, weight, out):
             nc.sync.dma_start(out=out_view[b][:, :, n], in_=out_sb[b][:, :, n])
 
         ALL = [0, 1, 2, 3]
-        for h in range(2):
-            w_split(nc.vector.tensor_copy, h, 0, 2, 0)
-            w_split(nc.scalar.copy, h, 0, 1, 2)
-        for s in range(OT):
-            w_transpose(s)
+        EVEN = [0, 2]
+        ODD = [1, 3]
+        w_split(nc.vector.tensor_copy, 0, 0, 2)
+        w_split(nc.scalar.copy, 1, 1, 2)
+        w_split(nc.vector.tensor_copy, 1, 0, 1)
+        w_transpose(0)
+        w_transpose(1)
         add(0, W)
         w_quant(0)
         w_quant(1)
-        w_move(0, 2)
+        w_move()
+        for i in range(EARLY, len(LOADS)):
+            load_x(i)
         quant(0)
-        bank(0, 0, [0, 1])
-        bank(0, 1, [0, 1])
+        w_keep()
         help_add(128)
-        w_quant(2)
-        w_quant(3)
         help_add(192)
-        w_move(2, 4)
-        add(256, W)
-        bank(0, 0, [2, 3])
-        store(0, 0, 1)
-        bank(0, 1, [2, 3])
-        store(1, 0, 1)
-        add(448, 64)
         quant(1)
-        help_add(384)
-        bank(1, 0, ALL)
-        bank(1, 1, ALL)
+        bank(0, 0, EVEN)
+        bank(0, 1, ODD)
+        help_add(256)
+        add(320, 64)
+        add(384, W)
+        bank(0, 0, ODD)
+        bank(0, 1, EVEN)
         quant(2)
-        for u in range(2, NU - 1):
-            if u < NU - 3:
+        quant(3)
+        for b in range(BATCH):
+            bank(1, b, ALL)
+            store(b, 0, 2)
+        for u in range(2, NU):
+            if u < NU - 2:
                 add((u + 2) * W, W)
-            elif u == NU - 3:
-                add((u + 2) * W, W // 2)
-            else:
-                add((u + 1) * W + W // 2, W // 2)
-            quant(u + 1)
-            bank(u, 0, ALL, u == NU - 2)
-            if u % 2 == 0:
-                store(0, u - 1, u + 1)
-            bank(u, 1, ALL)
-            if u % 2 == 0:
-                store(1, u - 1, u + 1)
-        bank(NU - 1, 0, ALL, True)
-        store(0, NU - 1, NU)
-        bank(NU - 1, 1, ALL)
-        store(1, NU - 1, NU)
+            if 4 <= u + 1 < NU:
+                quant(u + 1)
+            for b in range(BATCH):
+                bank(u, b, ALL, b == 0 and u >= NU - 2)
+                if u % 2 == 1:
+                    store(b, u - 1, u + 1)

@@ -23,11 +23,14 @@ INV = 1.0 / 16.0
 
 W = 128
 NU = NPOS // W
-LOADS = [(0, 128), (128, 128), (256, 256), (512, 128), (640, 128), (768, 256)]
-EARLY = 4
+LOADS = [(0, 128), (128, 256), (384, 256), (640, 128), (768, 256)]
+EARLY = 3
 HW = 64
 CW = 2 * P
 SW = CW + CW // 4
+
+
+STORE_AFTER = [(1, 0), (2, 1), (4, 0), (5, 1), (7, 0), (7, 1)]
 
 
 def tile_nonoverlappingconv1d_shared_kernel(tc, x, weight, out):
@@ -191,9 +194,13 @@ def tile_nonoverlappingconv1d_shared_kernel(tc, x, weight, out):
             else:
                 nc.scalar.activation(out=dst, in_=srcv, func=COPY, scale=INV)
 
-        def store(b, u0, u1):
-            n = slice(u0 * W, u1 * W)
-            nc.sync.dma_start(out=out_view[b][:, :, n], in_=out_sb[b][:, :, n])
+        stored = [0, 0]
+
+        def store(u, b):
+            if (u, b) in STORE_AFTER:
+                n = slice(stored[b] * W, (u + 1) * W)
+                nc.sync.dma_start(out=out_view[b][:, :, n], in_=out_sb[b][:, :, n])
+                stored[b] = u + 1
 
         ALL = [0, 1, 2, 3]
         EVEN = [0, 2]
@@ -211,27 +218,29 @@ def tile_nonoverlappingconv1d_shared_kernel(tc, x, weight, out):
             load_x(i)
         quant(0)
         w_keep()
-        help_add(128)
-        help_add(192)
-        quant(1)
-        bank(0, 0, EVEN)
-        bank(0, 1, ODD)
         help_add(256)
-        add(320, 64)
-        add(384, W)
+        add(128, W)
+        bank(0, 0, EVEN)
+        help_add(320)
+        bank(0, 1, ODD)
+        add(384, 64)
+        quant(1)
+        quant(2)
         bank(0, 0, ODD)
         bank(0, 1, EVEN)
-        quant(2)
+        bank(1, 0, ALL)
+        store(1, 0)
+        help_add(512)
+        bank(1, 1, ALL)
+        store(1, 1)
+        add(448, 64)
+        add(576, 64)
         quant(3)
-        for b in range(BATCH):
-            bank(1, b, ALL)
-            store(b, 0, 2)
         for u in range(2, NU):
-            if u < NU - 2:
-                add((u + 2) * W, W)
-            if 4 <= u + 1 < NU:
-                quant(u + 1)
+            if 5 <= u + 3 < NU:
+                add((u + 3) * W, W)
+            if u + 2 < NU:
+                quant(u + 2)
             for b in range(BATCH):
                 bank(u, b, ALL, b == 0 and u >= NU - 2)
-                if u % 2 == 1:
-                    store(b, u - 1, u + 1)
+                store(u, b)

@@ -77,8 +77,8 @@ def tile_nonoverlappingconv1d_shared_kernel(tc, x, weight, out):
         w_q = keep.tile([P, 2 * SW], U32, name="w_q", align_bytes=64)
         for j in range(2):
             nc.vector.memset(w_q[:, j * SW + CW : (j + 1) * SW].bitcast(I32), 0)
-        nc.gpsimd.memset(w_lo[HALF:P, :].bitcast(I32), 0)
-        nc.gpsimd.memset(w_hi[0:HALF, :].bitcast(I32), 0)
+        nc.vector.memset(w_lo[HALF:P, :].bitcast(I32), 0)
+        nc.vector.memset(w_hi[0:HALF, :].bitcast(I32), 0)
 
         wk = [keep.tile([P, 2, 2 * CH], BF16, name="wk%d" % j) for j in range(2)]
 

@@ -23,8 +23,8 @@ INV = 1.0 / 16.0
 
 W = 128
 NU = NPOS // W
-LOADS = [(0, 128), (128, 256), (384, 256), (640, 128), (768, 256)]
-EARLY = 3
+LOADS = [(0, 128), (128, 128), (256, 256), (512, 128), (640, 128), (768, 256)]
+EARLY = 4
 HW = 64
 CW = 2 * P
 SW = CW + CW // 4
@@ -218,29 +218,29 @@ def tile_nonoverlappingconv1d_shared_kernel(tc, x, weight, out):
             load_x(i)
         quant(0)
         w_keep()
-        help_add(256)
-        add(128, W)
-        bank(0, 0, EVEN)
-        help_add(320)
-        bank(0, 1, ODD)
-        add(384, 64)
+        help_add(128)
+        help_add(192)
         quant(1)
+        bank(0, 0, EVEN)
+        bank(0, 1, ODD)
+        help_add(256)
+        add(320, 64)
+        add(384, W)
+        bank(1, 0, EVEN)
+        bank(1, 1, ODD)
         quant(2)
-        bank(0, 0, ODD)
-        bank(0, 1, EVEN)
-        bank(1, 0, ALL)
-        store(1, 0)
-        help_add(512)
-        bank(1, 1, ALL)
-        store(1, 1)
-        add(448, 64)
-        add(576, 64)
         quant(3)
+        bank(0, 0, ODD)
+        bank(1, 0, ODD)
+        store(1, 0)
+        bank(0, 1, EVEN)
+        bank(1, 1, EVEN)
+        store(1, 1)
         for u in range(2, NU):
-            if 5 <= u + 3 < NU:
-                add((u + 3) * W, W)
-            if u + 2 < NU:
-                quant(u + 2)
+            if u < NU - 2:
+                add((u + 2) * W, W)
+            if 4 <= u + 1 < NU:
+                quant(u + 1)
             for b in range(BATCH):
                 bank(u, b, ALL, b == 0 and u >= NU - 2)
                 store(u, b)

from contextlib import ExitStack

import concourse.mybir as mybir
from concourse.masks import make_identity

BF16 = mybir.dt.bfloat16
F32 = mybir.dt.float32
U32 = mybir.dt.uint32
I32 = mybir.dt.int32
U8 = mybir.dt.uint8
FP8X4 = mybir.dt.float8_e4m3fn_x4
ADD = mybir.AluOpType.add
COPY = mybir.ActivationFunctionType.Copy

P = 128
HALF = 64
BATCH, CH, POS, OUTC = 2, 256, 4096, 512
NPOS = POS // 4
T = 4
OT = OUTC // P
FLOPS = 2 * BATCH * NPOS * (2 * CH) * OUTC
INV = 1.0 / 16.0

W = 128
NU = NPOS // W
LOADS = [(0, 128), (128, 128), (256, 256), (512, 128), (640, 128), (768, 256)]
EARLY = 4
HW = 64
CW = 2 * P
SW = CW + CW // 4


STORE_AFTER = [(1, 0), (2, 1), (4, 0), (5, 1), (7, 0), (7, 1)]


def tile_nonoverlappingconv1d_shared_kernel(tc, x, weight, out):
    nc = tc.nc
    with ExitStack() as ctx:
        ctx.enter_context(tc.manual_schedule())
        keep = ctx.enter_context(tc.tile_pool(name="keep", bufs=1))
        psum_w = ctx.enter_context(tc.psum_pool(name="psum_w", bufs=2))
        psum = ctx.enter_context(tc.psum_pool(name="psum", bufs=6))

        w_sb = keep.tile([P, OT * 2 * CH], BF16, name="w_sb")
        w_view = weight.rearrange("(p a) c one k -> p (a c one k)", a=OT)
        for h in range(2):
            cols = slice(h * OT * CH, (h + 1) * OT * CH)
            nc.sync.dma_start(out=w_sb[:, cols], in_=w_view[:, cols])
        x_view = x.rearrange("b (q t) d -> (b q) t d", t=T)
        x_tiles = []
        for i, (n0, w) in enumerate(LOADS):
            xt = keep.tile([P, T, 4 * w], BF16, name="x%d" % i)
            x_tiles.append(xt)

        def load_x(i):
            n0, w = LOADS[i]
            nc.sync.dma_start(out=x_tiles[i][:], in_=x_view[:, :, 4 * n0 : 4 * (n0 + w)])

        for i in range(EARLY):
            load_x(i)

        def x_part(n0, w):
            i = [j for j, (l0, lw) in enumerate(LOADS) if l0 <= n0 < l0 + lw][0]
            off = 4 * (n0 - LOADS[i][0])
            return x_tiles[i][:, :, off : off + 4 * w]

        ident = keep.tile([P, P], F32, name="ident")
        make_identity(nc, ident[:])
        ident_b = keep.tile([P, P], BF16, name="ident_b")
        make_identity(nc, ident_b[:])
        warm_in = keep.tile([P, 1], F32, name="warm_in")
        warm_out = keep.tile([P, 1], F32, name="warm_out")
        nc.vector.memset(warm_in[:], 0.0)
        nc.scalar.activation(out=warm_out[:], in_=warm_in[:], func=COPY, scale=1.0)
        w_lo = keep.tile([P, OT * SW], U32, name="w_lo", align_bytes=64)
        w_hi = keep.tile([P, OT * SW], U32, name="w_hi", align_bytes=64)
        w_q = keep.tile([P, 2 * SW], U32, name="w_q", align_bytes=64)
        for j in range(2):
            nc.vector.memset(w_q[:, j * SW + CW : (j + 1) * SW].bitcast(I32), 0)
        nc.vector.memset(w_lo[HALF:P, :].bitcast(I32), 0)
        nc.vector.memset(w_hi[0:HALF, :].bitcast(I32), 0)

        wk = [keep.tile([P, 2, 2 * CH], BF16, name="wk%d" % j) for j in range(2)]

        def w_split(copy, j, t0, t1):
            copy(
                out=wk[j][:, :, t0 * CH : t1 * CH],
                in_=w_sb[:, (2 * j + t0) * 2 * CH : (2 * j + t1) * 2 * CH].rearrange("p (c k) -> p k c", k=2),
            )

        w_grouped = keep.tile([P, 2 * 4 * CW], BF16, name="w_grouped", align_bytes=64)
        wg_words = w_grouped[:].bitcast(F32)

        def w_transpose(j):
            words = wk[j][:].rearrange("p k c -> p (k c)").bitcast(F32)
            wT = psum_w.tile([P, 512], F32, name="wT")
            for k in range(2):
                for e in range(2):
                    c0 = k * 2 * P + e
                    col = (2 * k + e) * P
                    nc.tensor.transpose(wT[:, col : col + P], words[:, c0 : c0 + 2 * P - 1 : 2], ident[:])
            nc.scalar.copy(
                out=wg_words[:, j * 512 : (j + 1) * 512].rearrange("p (k o e) -> p k o e", k=2, e=2),
                in_=wT[:].rearrange("p (k e o) -> p k o e", k=2, e=2),
            )

        def w_quant(j):
            nc.vector.quantize_mx(
                out=w_q[:, j * SW : j * SW + CW].bitcast(FP8X4),
                scales=w_q[:, j * SW + CW : (j + 1) * SW].bitcast(U8),
                in_=w_grouped[:, j * 4 * CW : (j + 1) * 4 * CW],
            )

        def w_move():
            even = slice(0, 2 * SW)
            odd = slice(2 * SW, 4 * SW)
            nc.sync.dma_start(out=w_lo[0:HALF, odd].bitcast(I32), in_=w_q[HALF:P, :].bitcast(I32))
            nc.sync.dma_start(out=w_hi[HALF:P, even].bitcast(I32), in_=w_q[0:HALF, :].bitcast(I32))

        def w_keep():
            even = slice(0, 2 * SW)
            odd = slice(2 * SW, 4 * SW)
            nc.vector.tensor_copy(out=w_lo[0:HALF, even].bitcast(I32), in_=w_q[0:HALF, :].bitcast(I32))
            nc.vector.tensor_copy(out=w_hi[HALF:P, odd].bitcast(I32), in_=w_q[HALF:P, :].bitcast(I32))

        def w_slot(b, a):
            return (w_lo if b == 0 else w_hi), 2 * (a % 2) + a // 2

        out_sb = [keep.tile([P, OT, NPOS], F32, name="out_sb%d" % b) for b in range(BATCH)]
        out_view = [out[b].rearrange("(p a) n -> p a n", a=OT) for b in range(BATCH)]
        grouped = []
        codes = []
        scales = []
        for u in range(NU):
            g = keep.tile([P, 2 * W * T], BF16, name="g%d" % u, align_bytes=64)
            c = keep.tile([P, 2 * W], U32, name="c%d" % u, align_bytes=64)
            s = keep.tile([P, 2 * W], U8, name="s%d" % u, align_bytes=64)
            grouped.append(g)
            codes.append(c)
            scales.append(s)

        def add(n0, w):
            u, i = divmod(n0, W)
            src = x_part(n0, w).rearrange("p t (n k e) -> p n t k e", k=2, e=2)
            nc.vector.tensor_tensor(
                out=grouped[u][:].rearrange("p (k n t) -> p n t k", k=2, t=T)[:, i : i + w],
                in0=src[:, :, :, :, 0],
                in1=src[:, :, :, :, 1],
                op=ADD,
            )

        def help_add(n0):
            u, i = divmod(n0, W)
            hb = psum_w.tile([P, 512], F32, name="wT")
            src = x_part(n0, HW).rearrange("p t (m e) -> p t m e", e=2)
            for t in range(T):
                for e in range(2):
                    nc.tensor.matmul(
                        out=hb[:, t * 2 * HW : (t + 1) * 2 * HW],
                        lhsT=ident_b[:],
                        rhs=src[:, t, :, e],
                        start=(e == 0),
                        stop=(e == 1),
                    )
            nc.scalar.copy(
                out=grouped[u][:].rearrange("p (k n t) -> p n t k", k=2, t=T)[:, i : i + HW],
                in_=hb[:].rearrange("p (t n k) -> p n t k", t=T, k=2),
            )

        def quant(u):
            nc.vector.quantize_mx(out=codes[u][:].bitcast(FP8X4), scales=scales[u][:], in_=grouped[u][:])

        def bank(u, b, tiles, on_vector=False):
            acc = psum.tile([P, 512], F32, name="acc")
            for j, a in enumerate(tiles):
                wt, s = w_slot(b, a)
                base = s * SW
                sc = wt[:, base + CW : base + SW].bitcast(U8)
                for k in range(2):
                    nc.tensor.matmul_mx(
                        out=acc[:, j * W : (j + 1) * W],
                        lhsT=wt[:, base + k * P : base + (k + 1) * P].bitcast(FP8X4),
                        lhsT_scale=sc[:, k * P : (k + 1) * P],
                        rhs=codes[u][:, k * W : (k + 1) * W].bitcast(FP8X4),
                        rhs_scale=scales[u][:, k * W : (k + 1) * W],
                        start=(k == 0),
                        stop=(k == 1),
                    )
            step = tiles[1] - tiles[0]
            dst = out_sb[b][:, tiles[0] : tiles[-1] + 1 : step, u * W : (u + 1) * W]
            srcv = acc[:, : len(tiles) * W].rearrange("p (a n) -> p a n", n=W)
            if on_vector:
                nc.vector.tensor_scalar_mul(out=dst, in0=srcv, scalar1=INV)
            else:
                nc.scalar.activation(out=dst, in_=srcv, func=COPY, scale=INV)

        stored = [0, 0]

        def store(u, b):
            if (u, b) in STORE_AFTER:
                n = slice(stored[b] * W, (u + 1) * W)
                nc.sync.dma_start(out=out_view[b][:, :, n], in_=out_sb[b][:, :, n])
                stored[b] = u + 1

        ALL = [0, 1, 2, 3]
        EVEN = [0, 2]
        ODD = [1, 3]
        w_split(nc.vector.tensor_copy, 0, 0, 2)
        w_split(nc.scalar.copy, 1, 1, 2)
        w_split(nc.vector.tensor_copy, 1, 0, 1)
        w_transpose(0)
        w_transpose(1)
        add(0, W)
        w_quant(0)
        w_quant(1)
        w_move()
        for i in range(EARLY, len(LOADS)):
            load_x(i)
        quant(0)
        w_keep()
        help_add(128)
        help_add(192)
        quant(1)
        bank(0, 0, EVEN)
        bank(0, 1, ODD)
        help_add(256)
        add(320, 64)
        add(384, W)
        bank(1, 0, EVEN)
        bank(1, 1, ODD)
        quant(2)
        quant(3)
        bank(0, 0, ODD)
        bank(1, 0, ODD)
        store(1, 0)
        bank(0, 1, EVEN)
        bank(1, 1, EVEN)
        store(1, 1)
        for u in range(2, NU):
            if u < NU - 2:
                add((u + 2) * W, W)
            if 4 <= u + 1 < NU:
                quant(u + 1)
            for b in range(BATCH):
                bank(u, b, ALL, b == 0 and u >= NU - 2)
                store(u, b)
